import numpy as np
import ml_dtypes


def mxq(x, axis, fmt="e4m3"):
    dtype, down = {"e4m3": (ml_dtypes.float8_e4m3fn, 7), "e5m2": (ml_dtypes.float8_e5m2, 14)}[fmt]
    v = np.moveaxis(np.asarray(x, np.float32).astype(ml_dtypes.bfloat16).astype(np.float64), axis, -1)
    blocks = v.reshape(v.shape[:-1] + (-1, 32))
    amax = np.abs(blocks).max(-1, keepdims=True)
    byte = np.maximum(np.where(amax > 0, np.frexp(amax)[1] - 1 + 127, 0) - down, 1)
    scale = np.exp2(byte - 127.0)
    codes = (blocks / scale).astype(np.float32).astype(dtype).astype(np.float64)
    return np.moveaxis((codes * scale).reshape(v.shape), -1, axis)


WIDE = False


def mx_kscale(k):
    if not WIDE:
        return np.ones(k)
    levels = np.array([10, -10, 5, -5, 0])
    a = np.random.permutation(np.resize(levels, k // 512 * 4)).reshape(k // 512, 4)
    idx = np.arange(k)
    return np.exp2(a[idx // 512, idx % 128 // 32])


BF16 = ml_dtypes.bfloat16


def bf(x):
    return np.asarray(x, np.float32).astype(BF16)


def f64(x):
    return np.asarray(x).astype(np.float64)


B, DIN, DOUT = 512, 1024, 1024


def sigmoid(v):
    return 1.0 / (1.0 + np.exp(-v))


def setup_inputs():
    s, t = mx_kscale(DIN), mx_kscale(DOUT)
    inp = {"x": bf(np.random.standard_normal((B, DIN)) * s),
           "h": bf(np.random.standard_normal((B, DOUT)) * t),
           "c": bf(np.random.standard_normal((B, DOUT)))}
    for n in "ifgo":
        inp["Wx" + n] = bf(np.random.standard_normal((DIN, DOUT)) * 0.7 / np.sqrt(DIN) / s[:, None])
        inp["Wh" + n] = bf(np.random.standard_normal((DOUT, DOUT)) * 0.7 / np.sqrt(DOUT) / t[:, None])
        inp["bx" + n] = bf(np.random.standard_normal(DOUT) * 0.3)
        inp["bh" + n] = bf(np.random.standard_normal(DOUT) * 0.3)
    return inp


def reference(x, h, c,
              Wxi, Whi, bxi, bhi,
              Wxf, Whf, bxf, bhf,
              Wxg, Whg, bxg, bhg,
              Wxo, Who, bxo, bho):
    Wx = np.concatenate([f64(Wxi), f64(Wxf), f64(Wxg), f64(Wxo)], axis=1)
    Wh = np.concatenate([f64(Whi), f64(Whf), f64(Whg), f64(Who)], axis=1)
    b = np.concatenate([f64(bxi) + f64(bhi), f64(bxf) + f64(bhf), f64(bxg) + f64(bhg), f64(bxo) + f64(bho)])
    z = (mxq(f64(x), 1, "e4m3") @ mxq(Wx, 0, "e4m3")) + (mxq(f64(h), 1, "e4m3") @ mxq(Wh, 0, "e4m3")) + b
    zi, zf, zg, zo = np.split(z, 4, axis=1)
    i = sigmoid(zi)
    f = sigmoid(zf)
    g = np.tanh(zg)
    o = sigmoid(zo)
    c_new = f * f64(c) + i * g
    h_new = o * np.tanh(c_new)
    return (h_new, c_new)

@@ -1,0 +1,281 @@
+from contextlib import ExitStack
+
+import concourse.mybir as mybir
+from concourse.masks import make_identity
+
+F32 = mybir.dt.float32
+BF16 = mybir.dt.bfloat16
+U32 = mybir.dt.uint32
+U8 = mybir.dt.uint8
+FP8X4 = mybir.dt.float8_e4m3fn_x4
+ACT = mybir.ActivationFunctionType
+
+P = 128
+PACK = 4
+K_PASS = P * PACK
+BATCH = 512
+DIM = 1024
+BATCH_TILES = BATCH // P
+PASSES = 2 * DIM // K_PASS
+GATE_I, GATE_F, GATE_G, GATE_O = 0, 1, 2, 3
+GATES = 4
+CHUNKS = GATES * PASSES
+HALF = DIM // 2
+HALF_TILES = HALF // P
+HALVES = 2 * GATES
+UNITS = HALVES * PASSES
+VECTOR_COLUMNS = 256
+RAW_BUFFERS = 12
+STORE_TILES = 2
+FINISH_STEPS = 4
+
+FLOPS = 2 * BATCH * 2 * DIM * GATES * DIM
+
+
+def tile_lstmcell_kernel(
+    tc, x, h, c,
+    wxi, whi, bxi, bhi,
+    wxf, whf, bxf, bhf,
+    wxg, whg, bxg, bhg,
+    wxo, who, bxo, bho,
+    out_0, out_1,
+):
+    nc = tc.nc
+    gate_weights = [(wxi, whi), (wxf, whf), (wxg, whg), (wxo, who)]
+    gate_biases = [(bxi, bhi), (bxf, bhf), (bxg, bhg), (bxo, bho)]
+    gate_functions = [ACT.Sigmoid, ACT.Sigmoid, ACT.Tanh, ACT.Sigmoid]
+    h_new_rows = out_0.rearrange("(b p) n -> p b n", p=P)
+    c_new_rows = out_1.rearrange("(b p) n -> p b n", p=P)
+
+    with ExitStack() as stack:
+        keep = stack.enter_context(tc.tile_pool(name="keep", bufs=1))
+        raw_pool = stack.enter_context(tc.tile_pool(name="raw", bufs=RAW_BUFFERS))
+        grouped_pool = stack.enter_context(tc.tile_pool(name="grouped", bufs=4))
+        codes_pool = stack.enter_context(tc.tile_pool(name="codes", bufs=6))
+        gate_pool = stack.enter_context(tc.tile_pool(name="gate", bufs=8))
+        banks = stack.enter_context(tc.psum_pool(name="banks", bufs=8))
+        stack.enter_context(tc.manual_schedule())
+
+        identity = keep.tile([P, P], F32)
+        table_warmer = keep.tile([P, 1], F32)
+        bias_rows = keep.tile([P, 2, P], BF16)
+        bias_row_sums = keep.tile([P, P], F32)
+        bias_columns = keep.tile([P, GATES * DIM // P], F32)
+        moving_codes = keep.tile([P, PASSES, BATCH], U32, align_bytes=64)
+        moving_scales = keep.tile([P, PASSES, BATCH], U8, align_bytes=64)
+        c_rows = keep.tile([P, BATCH_TILES, DIM], BF16)
+        i_gate = keep.tile([P, DIM // P, BATCH], F32)
+        c_new = keep.tile([P, BATCH_TILES, DIM], F32)
+        h_new = keep.tile([P, BATCH_TILES, DIM], F32)
+
+        raw_chunks = {}
+        grouped_units = {}
+        stationary_units = {}
+        accumulators = {}
+        gate_tiles = {}
+        turned_banks = {}
+
+        def load_batch_rows(rows, source):
+            view = source.rearrange("(b p) k -> p b k", p=P)
+            for first in range(0, BATCH_TILES, 2):
+                nc.sync.dma_start(out=rows[:, first : first + 2, :], in_=view[:, first : first + 2, :])
+
+        def load_chunk(chunk):
+            gate, k_pass = divmod(chunk, PASSES)
+            weight = gate_weights[gate][k_pass // 2]
+            first_row = (k_pass % 2) * K_PASS
+            raw = raw_pool.tile([P, PACK, DIM], BF16, name="raw", tag="raw")
+            nc.sync.dma_start(
+                out=raw[:].rearrange("q (u e) n -> q u e n", u=2),
+                in_=weight[first_row : first_row + K_PASS, :].rearrange("(u q e) n -> q u e n", u=2, e=2),
+            )
+            raw_chunks[chunk] = raw
+
+        def quantise_moving(operand, rows):
+            words = rows[:].bitcast(F32)
+            for g in range(2):
+                grouped = grouped_pool.tile([P, BATCH, PACK], BF16, name="grouped", tag="grouped", align_bytes=64)
+                grouped_words = grouped[:].bitcast(F32)
+                for side in range(2):
+                    bank = banks.tile([P, 2, 2 * P], F32, name="bank", tag="bank")
+                    for u in range(2):
+                        for b in range(2):
+                            first_word = (K_PASS // 2) * g + P * u
+                            nc.tensor.transpose(
+                                out=bank[:, u, b * P : (b + 1) * P],
+                                in_=words[:, 2 * side + b, first_word : first_word + P],
+                                identity=identity[:],
+                            )
+                    copy = nc.vector.tensor_copy if side == 0 else nc.scalar.copy
+                    copy(
+                        out=grouped_words[:, side * 2 * P : (side + 1) * 2 * P, :],
+                        in_=bank[:].rearrange("q u b -> q b u"),
+                    )
+                k_pass = 2 * operand + g
+                nc.vector.quantize_mx(
+                    out=moving_codes[:, k_pass, :].bitcast(FP8X4),
+                    scales=moving_scales[:, k_pass, :],
+                    in_=grouped[:].rearrange("q b t -> q (b t)"),
+                )
+
+        def regroup_copy(copy, grouped_part, raw_part):
+            copy(
+                out=grouped_part.rearrange("q (n i) t -> q n t i", i=4),
+                in_=raw_part.rearrange("q t (n i) -> q n t i", i=4),
+            )
+
+        def regroup(unit):
+            half, k_pass = divmod(unit, PASSES)
+            raw = raw_chunks[(half // 2) * PASSES + k_pass]
+            first = (half % 2) * HALF
+            split = VECTOR_COLUMNS
+            grouped = grouped_pool.tile([P, HALF, PACK], BF16, name="grouped", tag="grouped", align_bytes=64)
+            regroup_copy(nc.vector.tensor_copy, grouped[:, 0:split, :], raw[:, :, first : first + split])
+            regroup_copy(nc.scalar.copy, grouped[:, split:HALF, :], raw[:, :, first + split : first + HALF])
+            grouped_units[unit] = grouped
+
+        def quantise(unit):
+            codes = codes_pool.tile([P, HALF], U32, name="codes", tag="codes", align_bytes=64)
+            scales = codes_pool.tile([P, HALF], U8, name="scales", tag="scales", align_bytes=64)
+            nc.vector.quantize_mx(
+                out=codes[:].bitcast(FP8X4),
+                scales=scales[:],
+                in_=grouped_units[unit][:].rearrange("q n t -> q (n t)"),
+            )
+            stationary_units[unit] = (codes, scales)
+
+        def multiply(unit):
+            half, k_pass = divmod(unit, PASSES)
+            codes, scales = stationary_units[unit]
+            for j in range(HALF_TILES):
+                if k_pass == 0:
+                    accumulators[(half, j)] = banks.tile([P, BATCH], F32, name="bank", tag="bank")
+                columns = slice(j * P, (j + 1) * P)
+                nc.tensor.matmul_mx(
+                    out=accumulators[(half, j)][:],
+                    lhsT=codes[:, columns].bitcast(FP8X4),
+                    lhsT_scale=scales[:, columns],
+                    rhs=moving_codes[:, k_pass, :].bitcast(FP8X4),
+                    rhs_scale=moving_scales[:, k_pass, :],
+                    start=(k_pass == 0),
+                    stop=(k_pass == PASSES - 1),
+                )
+
+        def activate(half, j):
+            gate = half // 2
+            tile_index = (half % 2) * HALF_TILES + j
+            if gate == GATE_I:
+                result = i_gate[:, tile_index, :]
+            else:
+                gate_tiles[(half, j)] = gate_pool.tile([P, BATCH], F32, name="gate_tile", tag="gate_tile")
+                result = gate_tiles[(half, j)][:]
+            bias_index = gate * (DIM // P) + tile_index
+            nc.scalar.activation(
+                out=result,
+                in_=accumulators[(half, j)][:],
+                func=gate_functions[gate],
+                bias=bias_columns[:, bias_index : bias_index + 1],
+                scale=1.0,
+            )
+
+        def multiply_by_i(half, j):
+            g_tile = gate_tiles[(half, j)]
+            nc.vector.tensor_mul(out=g_tile[:], in0=g_tile[:], in1=i_gate[:, (half % 2) * HALF_TILES + j, :])
+
+        def turn(half, j):
+            bank = banks.tile([P, BATCH_TILES, P], F32, name="bank", tag="bank")
+            for b in range(BATCH_TILES):
+                nc.tensor.transpose(
+                    out=bank[:, b, :],
+                    in_=gate_tiles[(half, j)][:, b * P : (b + 1) * P],
+                    identity=identity[:],
+                )
+            turned_banks[(half, j)] = bank
+
+        def first_column(half, j):
+            return (half % 2) * HALF + j * P
+
+        def combine(half, j):
+            gate = half // 2
+            first = first_column(half, j)
+            columns = slice(first, first + P)
+            turned = turned_banks[(half, j)][:]
+            if gate == GATE_F:
+                nc.vector.tensor_mul(out=c_new[:, :, columns], in0=turned, in1=c_rows[:, :, columns])
+            if gate == GATE_G:
+                nc.vector.tensor_add(out=c_new[:, :, columns], in0=turned, in1=c_new[:, :, columns])
+            if gate == GATE_O:
+                nc.vector.tensor_mul(out=h_new[:, :, columns], in0=turned, in1=h_new[:, :, columns])
+            if j % STORE_TILES == STORE_TILES - 1:
+                piece = slice(first + P - STORE_TILES * P, first + P)
+                if gate == GATE_G:
+                    nc.sync.dma_start(out=c_new_rows[:, :, piece], in_=c_new[:, :, piece])
+                if gate == GATE_O:
+                    nc.sync.dma_start(out=h_new_rows[:, :, piece], in_=h_new[:, :, piece])
+
+        def tanh_of_c_new(half, j):
+            first = first_column(half, j)
+            columns = slice(first, first + P)
+            nc.scalar.activation(out=h_new[:, :, columns], in_=c_new[:, :, columns], func=ACT.Tanh)
+
+        def finish(half, j, step):
+            gate = half // 2
+            if step == 0:
+                activate(half, j)
+            if gate == GATE_G:
+                if step == 1:
+                    multiply_by_i(half, j)
+                if step == 2:
+                    turn(half, j)
+                    combine(half, j)
+                if step == 3:
+                    tanh_of_c_new(half, j)
+            if gate in (GATE_F, GATE_O) and step == 1:
+                turn(half, j)
+                combine(half, j)
+
+        make_identity(nc, identity[:])
+        x_rows = raw_pool.tile([P, BATCH_TILES, DIM], BF16, name="raw", tag="raw")
+        h_rows = raw_pool.tile([P, BATCH_TILES, DIM], BF16, name="raw", tag="raw")
+        load_batch_rows(x_rows, x)
+        nc.vector.memset(bias_rows[:], 0.0)
+        for gate in range(GATES):
+            for source in range(2):
+                nc.scalar.dma_start(
+                    out=bias_rows[gate * (DIM // P) : (gate + 1) * (DIM // P), source, :],
+                    in_=gate_biases[gate][source].rearrange("(d p) -> d p", p=P),
+                )
+        load_batch_rows(h_rows, h)
+        for chunk in range(2 * PASSES):
+            load_chunk(chunk)
+        load_batch_rows(c_rows, c)
+        for chunk in range(2 * PASSES, RAW_BUFFERS - 2):
+            load_chunk(chunk)
+
+        nc.scalar.activation(out=table_warmer[:], in_=identity[:, 0:1], func=ACT.Sigmoid)
+
+        quantise_moving(0, x_rows)
+        quantise_moving(1, h_rows)
+        for chunk in range(RAW_BUFFERS - 2, RAW_BUFFERS):
+            load_chunk(chunk)
+
+        nc.vector.tensor_add(out=bias_row_sums[:], in0=bias_rows[:, 0, :], in1=bias_rows[:, 1, :])
+        bias_bank = banks.tile([P, P], F32, name="bank", tag="bank")
+        nc.tensor.transpose(out=bias_bank[:], in_=bias_row_sums[:], identity=identity[:])
+        nc.vector.tensor_copy(out=bias_columns[:], in_=bias_bank[:, 0 : GATES * DIM // P])
+
+        for r in range(UNITS + 2 + HALF_TILES + FINISH_STEPS):
+            if r < UNITS:
+                regroup(r)
+                half, k_pass = divmod(r, PASSES)
+                next_chunk = RAW_BUFFERS + (half // 2) * PASSES + k_pass
+                if half % 2 == 1 and next_chunk < CHUNKS:
+                    load_chunk(next_chunk)
+            if 1 <= r <= UNITS:
+                quantise(r - 1)
+            for half in range(HALVES):
+                last_unit = half * PASSES + PASSES - 1
+                for j in range(HALF_TILES):
+                    finish(half, j, r - (last_unit + 2 + j))
+            if 1 <= r <= UNITS:
+                multiply(r - 1)

@@ -54,7 +54,6 @@ def tile_lstmcell_kernel(
         codes_pool = stack.enter_context(tc.tile_pool(name="codes", bufs=6))
         gate_pool = stack.enter_context(tc.tile_pool(name="gate", bufs=8))
         banks = stack.enter_context(tc.psum_pool(name="banks", bufs=8))
-        stack.enter_context(tc.manual_schedule())
 
         identity = keep.tile([P, P], F32)
         table_warmer = keep.tile([P, 1], F32)
@@ -67,6 +66,18 @@ def tile_lstmcell_kernel(
         i_gate = keep.tile([P, DIM // P, BATCH], F32)
         c_new = keep.tile([P, BATCH_TILES, DIM], F32)
         h_new = keep.tile([P, BATCH_TILES, DIM], F32)
+
+        units = []
+        for k_pass in range(PASSES):
+            for half in range(2):
+                units.append((half, k_pass))
+        for half in range(2, HALVES):
+            for k_pass in range(PASSES):
+                units.append((half, k_pass))
+        last_unit = {}
+        for position, (half, k_pass) in enumerate(units):
+            if k_pass == PASSES - 1:
+                last_unit[half] = position
 
         raw_chunks = {}
         grouped_units = {}
@@ -125,7 +136,7 @@ def tile_lstmcell_kernel(
             )
 
         def regroup(unit):
-            half, k_pass = divmod(unit, PASSES)
+            half, k_pass = units[unit]
             raw = raw_chunks[(half // 2) * PASSES + k_pass]
             first = (half % 2) * HALF
             split = VECTOR_COLUMNS
@@ -145,7 +156,7 @@ def tile_lstmcell_kernel(
             stationary_units[unit] = (codes, scales)
 
         def multiply(unit):
-            half, k_pass = divmod(unit, PASSES)
+            half, k_pass = units[unit]
             codes, scales = stationary_units[unit]
             for j in range(HALF_TILES):
                 if k_pass == 0:
@@ -235,6 +246,8 @@ def tile_lstmcell_kernel(
                 combine(half, j)
 
         make_identity(nc, identity[:])
+        nc.vector.memset(table_warmer[:], 0.0)
+        nc.scalar.activation(out=table_warmer[:], in_=table_warmer[:], func=ACT.Sigmoid)
         x_rows = raw_pool.tile([P, BATCH_TILES, DIM], BF16, name="raw", tag="raw")
         h_rows = raw_pool.tile([P, BATCH_TILES, DIM], BF16, name="raw", tag="raw")
         load_batch_rows(x_rows, x)
@@ -252,8 +265,6 @@ def tile_lstmcell_kernel(
         for chunk in range(2 * PASSES, RAW_BUFFERS - 2):
             load_chunk(chunk)
 
-        nc.scalar.activation(out=table_warmer[:], in_=identity[:, 0:1], func=ACT.Sigmoid)
-
         quantise_moving(0, x_rows)
         quantise_moving(1, h_rows)
         for chunk in range(RAW_BUFFERS - 2, RAW_BUFFERS):
@@ -267,15 +278,15 @@ def tile_lstmcell_kernel(
         for r in range(UNITS + 2 + HALF_TILES + FINISH_STEPS):
             if r < UNITS:
                 regroup(r)
-                half, k_pass = divmod(r, PASSES)
+                half, k_pass = units[r]
                 next_chunk = RAW_BUFFERS + (half // 2) * PASSES + k_pass
                 if half % 2 == 1 and next_chunk < CHUNKS:
                     load_chunk(next_chunk)
             if 1 <= r <= UNITS:
                 quantise(r - 1)
             for half in range(HALVES):
-                last_unit = half * PASSES + PASSES - 1
+                tiles_a_round = 2 if half // 2 == GATE_I else 1
                 for j in range(HALF_TILES):
-                    finish(half, j, r - (last_unit + 2 + j))
+                    finish(half, j, r - (last_unit[half] + 2 + j // tiles_a_round))
             if 1 <= r <= UNITS:
                 multiply(r - 1)

@@ -24,9 +24,12 @@ HALF = DIM // 2
 HALF_TILES = HALF // P
 HALVES = 2 * GATES
 UNITS = HALVES * PASSES
+VECTOR_COLUMNS_EARLY = 320
 VECTOR_COLUMNS = 256
+GROUPED_TILES = 4
 RAW_BUFFERS = 12
 STORE_TILES = 2
+HEAD_ROUNDS = PASSES
 FINISH_STEPS = 4
 
 FLOPS = 2 * BATCH * 2 * DIM * GATES * DIM
@@ -50,7 +53,6 @@ def tile_lstmcell_kernel(
     with ExitStack() as stack:
         keep = stack.enter_context(tc.tile_pool(name="keep", bufs=1))
         raw_pool = stack.enter_context(tc.tile_pool(name="raw", bufs=RAW_BUFFERS))
-        grouped_pool = stack.enter_context(tc.tile_pool(name="grouped", bufs=4))
         codes_pool = stack.enter_context(tc.tile_pool(name="codes", bufs=6))
         gate_pool = stack.enter_context(tc.tile_pool(name="gate", bufs=8))
         banks = stack.enter_context(tc.psum_pool(name="banks", bufs=8))
@@ -68,16 +70,17 @@ def tile_lstmcell_kernel(
         h_new = keep.tile([P, BATCH_TILES, DIM], F32)
 
         units = []
-        for k_pass in range(PASSES):
-            for half in range(2):
-                units.append((half, k_pass))
-        for half in range(2, HALVES):
+        for half in range(HALVES):
             for k_pass in range(PASSES):
                 units.append((half, k_pass))
         last_unit = {}
         for position, (half, k_pass) in enumerate(units):
             if k_pass == PASSES - 1:
                 last_unit[half] = position
+
+        grouped_ring = []
+        for slot in range(GROUPED_TILES):
+            grouped_ring.append(keep.tile([P, HALF, PACK], BF16, name="grouped%d" % slot, align_bytes=64))
 
         raw_chunks = {}
         grouped_units = {}
@@ -105,7 +108,7 @@ def tile_lstmcell_kernel(
         def quantise_moving(operand, rows):
             words = rows[:].bitcast(F32)
             for g in range(2):
-                grouped = grouped_pool.tile([P, BATCH, PACK], BF16, name="grouped", tag="grouped", align_bytes=64)
+                grouped = grouped_ring[(2 * operand + g) % GROUPED_TILES]
                 grouped_words = grouped[:].bitcast(F32)
                 for side in range(2):
                     bank = banks.tile([P, 2, 2 * P], F32, name="bank", tag="bank")
@@ -139,8 +142,8 @@ def tile_lstmcell_kernel(
             half, k_pass = units[unit]
             raw = raw_chunks[(half // 2) * PASSES + k_pass]
             first = (half % 2) * HALF
-            split = VECTOR_COLUMNS
-            grouped = grouped_pool.tile([P, HALF, PACK], BF16, name="grouped", tag="grouped", align_bytes=64)
+            split = VECTOR_COLUMNS_EARLY if half // 2 < GATE_G else VECTOR_COLUMNS
+            grouped = grouped_ring[unit % GROUPED_TILES]
             regroup_copy(nc.vector.tensor_copy, grouped[:, 0:split, :], raw[:, :, first : first + split])
             regroup_copy(nc.scalar.copy, grouped[:, split:HALF, :], raw[:, :, first + split : first + HALF])
             grouped_units[unit] = grouped
@@ -245,37 +248,13 @@ def tile_lstmcell_kernel(
                 turn(half, j)
                 combine(half, j)
 
-        make_identity(nc, identity[:])
-        nc.vector.memset(table_warmer[:], 0.0)
-        nc.scalar.activation(out=table_warmer[:], in_=table_warmer[:], func=ACT.Sigmoid)
-        x_rows = raw_pool.tile([P, BATCH_TILES, DIM], BF16, name="raw", tag="raw")
-        h_rows = raw_pool.tile([P, BATCH_TILES, DIM], BF16, name="raw", tag="raw")
-        load_batch_rows(x_rows, x)
-        nc.vector.memset(bias_rows[:], 0.0)
-        for gate in range(GATES):
-            for source in range(2):
-                nc.scalar.dma_start(
-                    out=bias_rows[gate * (DIM // P) : (gate + 1) * (DIM // P), source, :],
-                    in_=gate_biases[gate][source].rearrange("(d p) -> d p", p=P),
-                )
-        load_batch_rows(h_rows, h)
-        for chunk in range(2 * PASSES):
-            load_chunk(chunk)
-        load_batch_rows(c_rows, c)
-        for chunk in range(2 * PASSES, RAW_BUFFERS - 2):
-            load_chunk(chunk)
+        def prepare_biases():
+            nc.vector.tensor_add(out=bias_row_sums[:], in0=bias_rows[:, 0, :], in1=bias_rows[:, 1, :])
+            bias_bank = banks.tile([P, P], F32, name="bank", tag="bank")
+            nc.tensor.transpose(out=bias_bank[:], in_=bias_row_sums[:], identity=identity[:])
+            nc.vector.tensor_copy(out=bias_columns[:], in_=bias_bank[:, 0 : GATES * DIM // P])
 
-        quantise_moving(0, x_rows)
-        quantise_moving(1, h_rows)
-        for chunk in range(RAW_BUFFERS - 2, RAW_BUFFERS):
-            load_chunk(chunk)
-
-        nc.vector.tensor_add(out=bias_row_sums[:], in0=bias_rows[:, 0, :], in1=bias_rows[:, 1, :])
-        bias_bank = banks.tile([P, P], F32, name="bank", tag="bank")
-        nc.tensor.transpose(out=bias_bank[:], in_=bias_row_sums[:], identity=identity[:])
-        nc.vector.tensor_copy(out=bias_columns[:], in_=bias_bank[:, 0 : GATES * DIM // P])
-
-        for r in range(UNITS + 2 + HALF_TILES + FINISH_STEPS):
+        def pipeline_round(r):
             if r < UNITS:
                 regroup(r)
                 half, k_pass = units[r]
@@ -285,8 +264,38 @@ def tile_lstmcell_kernel(
             if 1 <= r <= UNITS:
                 quantise(r - 1)
             for half in range(HALVES):
-                tiles_a_round = 2 if half // 2 == GATE_I else 1
                 for j in range(HALF_TILES):
-                    finish(half, j, r - (last_unit[half] + 2 + j // tiles_a_round))
-            if 1 <= r <= UNITS:
-                multiply(r - 1)
+                    finish(half, j, r - (last_unit[half] + 3 + j))
+            if 2 <= r <= UNITS + 1:
+                multiply(r - 2)
+
+        with tc.manual_schedule():
+            make_identity(nc, identity[:])
+            nc.vector.memset(table_warmer[:], 0.0)
+            nc.scalar.activation(out=table_warmer[:], in_=table_warmer[:], func=ACT.Sigmoid)
+            x_rows = raw_pool.tile([P, BATCH_TILES, DIM], BF16, name="raw", tag="raw")
+            h_rows = raw_pool.tile([P, BATCH_TILES, DIM], BF16, name="raw", tag="raw")
+            load_batch_rows(x_rows, x)
+            nc.vector.memset(bias_rows[:], 0.0)
+            for gate in range(GATES):
+                for source in range(2):
+                    nc.scalar.dma_start(
+                        out=bias_rows[gate * (DIM // P) : (gate + 1) * (DIM // P), source, :],
+                        in_=gate_biases[gate][source].rearrange("(d p) -> d p", p=P),
+                    )
+            load_batch_rows(h_rows, h)
+            for chunk in range(2 * PASSES):
+                load_chunk(chunk)
+            load_batch_rows(c_rows, c)
+            for chunk in range(2 * PASSES, RAW_BUFFERS - 2):
+                load_chunk(chunk)
+            quantise_moving(0, x_rows)
+            quantise_moving(1, h_rows)
+            for chunk in range(RAW_BUFFERS - 2, RAW_BUFFERS):
+                load_chunk(chunk)
+            for r in range(HEAD_ROUNDS):
+                pipeline_round(r)
+            prepare_biases()
+
+        for r in range(HEAD_ROUNDS, UNITS + 3 + HALF_TILES + FINISH_STEPS):
+            pipeline_round(r)

@@ -296,6 +296,5 @@ def tile_lstmcell_kernel(
             for r in range(HEAD_ROUNDS):
                 pipeline_round(r)
             prepare_biases()
-
-        for r in range(HEAD_ROUNDS, UNITS + 3 + HALF_TILES + FINISH_STEPS):
-            pipeline_round(r)
+            for r in range(HEAD_ROUNDS, UNITS + 3 + HALF_TILES + FINISH_STEPS):
+                pipeline_round(r)

@@ -19,18 +19,29 @@ BATCH_TILES = BATCH // P
 PASSES = 2 * DIM // K_PASS
 GATE_I, GATE_F, GATE_G, GATE_O = 0, 1, 2, 3
 GATES = 4
-CHUNKS = GATES * PASSES
+TILES = DIM // P
 HALF = DIM // 2
-HALF_TILES = HALF // P
-HALVES = 2 * GATES
-UNITS = HALVES * PASSES
-VECTOR_COLUMNS_EARLY = 320
-VECTOR_COLUMNS = 256
-GROUPED_TILES = 4
-RAW_BUFFERS = 12
+
+GROUPS = [
+    (GATE_I, 0, 4),
+    (GATE_I, 4, 4),
+    (GATE_F, 0, 4),
+    (GATE_F, 4, 4),
+    (GATE_G, 0, 4),
+    (GATE_G, 4, 4),
+    (GATE_O, 0, 4),
+    (GATE_O, 4, 2),
+    (GATE_O, 6, 2),
+]
+RAW_BUFFERS = 7
+RAW_HALF_BUFFERS = 10
 STORE_TILES = 2
-HEAD_ROUNDS = PASSES
-FINISH_STEPS = 4
+PASS_BY_PASS = (0, 7, 8,)
+LAGS = [(2, 1, 1, 0), (2, 1, 1, 0), (2, 1, 1, 0), (2, 1, 1, 0), (2, 1, 1, 0), (2, 1, 1, 0), (2, 1, 1, 0), (2, 1, 1, 0), (2, 1, 1, 0)]
+ACT_SPACING = [1, 2, 2, 2, 2, 2, 2, 2, 2]
+VECTOR_SHARE = [256, 328, 256, 256, 256, 256, 256, 256, 256]
+COMBINE_FIRST = False
+EXTRA_ROUNDS = 4
 
 FLOPS = 2 * BATCH * 2 * DIM * GATES * DIM
 
@@ -53,84 +64,124 @@ def tile_lstmcell_kernel(
     with ExitStack() as stack:
         keep = stack.enter_context(tc.tile_pool(name="keep", bufs=1))
         raw_pool = stack.enter_context(tc.tile_pool(name="raw", bufs=RAW_BUFFERS))
-        codes_pool = stack.enter_context(tc.tile_pool(name="codes", bufs=6))
-        gate_pool = stack.enter_context(tc.tile_pool(name="gate", bufs=8))
-        banks = stack.enter_context(tc.psum_pool(name="banks", bufs=8))
+        raw_half_pool = stack.enter_context(tc.tile_pool(name="raw_half", bufs=RAW_HALF_BUFFERS))
+        grouped_pool = stack.enter_context(tc.tile_pool(name="grouped", bufs=5))
+        codes_pool = stack.enter_context(tc.tile_pool(name="codes", bufs=9))
+        gate_pool = stack.enter_context(tc.tile_pool(name="gate", bufs=7))
+        sum_banks = stack.enter_context(tc.psum_pool(name="sums", bufs=5))
+        turn_banks = stack.enter_context(tc.psum_pool(name="turns", bufs=3))
 
         identity = keep.tile([P, P], F32)
         table_warmer = keep.tile([P, 1], F32)
         bias_rows = keep.tile([P, 2, P], BF16)
         bias_row_sums = keep.tile([P, P], F32)
-        bias_columns = keep.tile([P, GATES * DIM // P], F32)
+        bias_columns = keep.tile([P, GATES * TILES], F32)
         moving_codes = keep.tile([P, PASSES, BATCH], U32, align_bytes=64)
         moving_scales = keep.tile([P, PASSES, BATCH], U8, align_bytes=64)
         c_rows = keep.tile([P, BATCH_TILES, DIM], BF16)
-        i_gate = keep.tile([P, DIM // P, BATCH], F32)
-        c_new = keep.tile([P, BATCH_TILES, DIM], F32)
-        h_new = keep.tile([P, BATCH_TILES, DIM], F32)
+        i_gate = keep.tile([P, TILES, BATCH], F32)
+        c_new = keep.tile([P, TILES // 2, BATCH_TILES, 2 * P], F32)
+        h_new = keep.tile([P, TILES // 2, BATCH_TILES, 2 * P], F32)
 
         units = []
-        for half in range(HALVES):
+        for k_pass in range(PASSES):
+            units += [(0, k_pass), (1, k_pass)]
+        for group in range(2, len(GROUPS)):
             for k_pass in range(PASSES):
-                units.append((half, k_pass))
-        last_unit = {}
-        for position, (half, k_pass) in enumerate(units):
-            if k_pass == PASSES - 1:
-                last_unit[half] = position
+                units.append((group, k_pass))
 
-        grouped_ring = []
-        for slot in range(GROUPED_TILES):
-            grouped_ring.append(keep.tile([P, HALF, PACK], BF16, name="grouped%d" % slot, align_bytes=64))
+        steps_in = {}
+
+        def plan(r, name, item):
+            steps_in.setdefault((r, name), []).append(item)
+
+        for group in range(len(GROUPS)):
+            gate, first_tile, tiles = GROUPS[group]
+            pass_lag, act_lag, turn_lag, combine_lag = LAGS[group]
+            last = units.index((group, PASSES - 1))
+            for j in range(tiles):
+                for k_pass in range(PASSES):
+                    if group in PASS_BY_PASS:
+                        plan(units.index((group, k_pass)) + pass_lag, "pass", (group, j, k_pass))
+                    else:
+                        plan(last + pass_lag + j, "pass", (group, j, k_pass))
+                if group == len(GROUPS) - 1:
+                    continue
+                r = last + pass_lag + act_lag + ACT_SPACING[group] * j // 2
+                plan(r, "act", (group, j))
+                if gate == GATE_G:
+                    plan(r + 1, "times_i", (group, j))
+                    r = r + 1
+                if gate != GATE_I:
+                    plan(r + turn_lag, "turn", (group, j))
+                    plan(r + turn_lag + combine_lag, "combine", (group, j))
+                if gate == GATE_G:
+                    plan(r + turn_lag + combine_lag + 1, "tanh", (group, j))
 
         raw_chunks = {}
         grouped_units = {}
-        stationary_units = {}
+        stationary = {}
         accumulators = {}
         gate_tiles = {}
         turned_banks = {}
 
-        def load_batch_rows(rows, source):
+        def load_batch_rows(rows, source, first):
             view = source.rearrange("(b p) k -> p b k", p=P)
-            for first in range(0, BATCH_TILES, 2):
-                nc.sync.dma_start(out=rows[:, first : first + 2, :], in_=view[:, first : first + 2, :])
+            nc.sync.dma_start(out=rows[:, first : first + 2, :], in_=view[:, first : first + 2, :])
+
+        def chunk_rows(chunk):
+            gate, k_pass = divmod(chunk, PASSES)
+            first_row = (k_pass % 2) * K_PASS
+            weight = gate_weights[gate][k_pass // 2]
+            return weight[first_row : first_row + K_PASS, :].rearrange("(q t) n -> q t n", t=PACK)
 
         def load_chunk(chunk):
-            gate, k_pass = divmod(chunk, PASSES)
-            weight = gate_weights[gate][k_pass // 2]
-            first_row = (k_pass % 2) * K_PASS
             raw = raw_pool.tile([P, PACK, DIM], BF16, name="raw", tag="raw")
-            nc.sync.dma_start(
-                out=raw[:].rearrange("q (u e) n -> q u e n", u=2),
-                in_=weight[first_row : first_row + K_PASS, :].rearrange("(u q e) n -> q u e n", u=2, e=2),
-            )
-            raw_chunks[chunk] = raw
+            nc.sync.dma_start(out=raw[:], in_=chunk_rows(chunk))
+            raw_chunks[(chunk, 0)] = raw[:, :, 0:HALF]
+            raw_chunks[(chunk, 1)] = raw[:, :, HALF:DIM]
 
-        def quantise_moving(operand, rows):
+        def load_half_chunk(chunk, half):
+            raw = raw_half_pool.tile([P, PACK, HALF], BF16, name="raw_half", tag="raw_half")
+            nc.sync.dma_start(out=raw[:], in_=chunk_rows(chunk)[:, :, half * HALF : (half + 1) * HALF])
+            raw_chunks[(chunk, half)] = raw[:]
+
+        def load_bias(index):
+            gate, source = divmod(index, 2)
+            nc.sync.dma_start(
+                out=bias_rows[gate * TILES : (gate + 1) * TILES, source, :],
+                in_=gate_biases[gate][source].rearrange("(d p) -> d p", p=P),
+            )
+
+        def turn_moving(rows, grouped, side):
             words = rows[:].bitcast(F32)
             for g in range(2):
-                grouped = grouped_ring[(2 * operand + g) % GROUPED_TILES]
-                grouped_words = grouped[:].bitcast(F32)
-                for side in range(2):
-                    bank = banks.tile([P, 2, 2 * P], F32, name="bank", tag="bank")
-                    for u in range(2):
-                        for b in range(2):
-                            first_word = (K_PASS // 2) * g + P * u
-                            nc.tensor.transpose(
-                                out=bank[:, u, b * P : (b + 1) * P],
-                                in_=words[:, 2 * side + b, first_word : first_word + P],
-                                identity=identity[:],
-                            )
-                    copy = nc.vector.tensor_copy if side == 0 else nc.scalar.copy
-                    copy(
-                        out=grouped_words[:, side * 2 * P : (side + 1) * 2 * P, :],
-                        in_=bank[:].rearrange("q u b -> q b u"),
-                    )
+                bank = turn_banks.tile([P, 2, 2 * P], F32, name="turned", tag="turned")
+                for u in range(2):
+                    for b in range(2):
+                        first_word = (K_PASS // 2) * g + u
+                        nc.tensor.transpose(
+                            out=bank[:, u, b * P : (b + 1) * P],
+                            in_=words[:, 2 * side + b, first_word : first_word + 2 * P - 1 : 2],
+                            identity=identity[:],
+                        )
+                copy = nc.vector.tensor_copy if side == 0 else nc.scalar.copy
+                copy(
+                    out=grouped[g][:].bitcast(F32)[:, side * 2 * P : (side + 1) * 2 * P, :],
+                    in_=bank[:].rearrange("q u b -> q b u"),
+                )
+
+        def quantise_moving(operand, grouped):
+            for g in range(2):
                 k_pass = 2 * operand + g
                 nc.vector.quantize_mx(
                     out=moving_codes[:, k_pass, :].bitcast(FP8X4),
                     scales=moving_scales[:, k_pass, :],
-                    in_=grouped[:].rearrange("q b t -> q (b t)"),
+                    in_=grouped[g][:].rearrange("q b t -> q (b t)"),
                 )
+
+        def grouped_tile():
+            return grouped_pool.tile([P, HALF, PACK], BF16, name="grouped", tag="grouped", align_bytes=64)
 
         def regroup_copy(copy, grouped_part, raw_part):
             copy(
@@ -138,163 +189,215 @@ def tile_lstmcell_kernel(
                 in_=raw_part.rearrange("q t (n i) -> q n t i", i=4),
             )
 
-        def regroup(unit):
-            half, k_pass = units[unit]
-            raw = raw_chunks[(half // 2) * PASSES + k_pass]
-            first = (half % 2) * HALF
-            split = VECTOR_COLUMNS_EARLY if half // 2 < GATE_G else VECTOR_COLUMNS
-            grouped = grouped_ring[unit % GROUPED_TILES]
-            regroup_copy(nc.vector.tensor_copy, grouped[:, 0:split, :], raw[:, :, first : first + split])
-            regroup_copy(nc.scalar.copy, grouped[:, split:HALF, :], raw[:, :, first + split : first + HALF])
+        def regroup(unit, split):
+            group, k_pass = units[unit]
+            gate, first_tile, tiles = GROUPS[group]
+            raw = raw_chunks[(gate * PASSES + k_pass, first_tile // (TILES // 2))]
+            first = first_tile * P % HALF
+            width = tiles * P
+            grouped = grouped_tile()
+            if split > 0:
+                regroup_copy(nc.vector.tensor_copy, grouped[:, 0:split, :], raw[:, :, first : first + split])
+            if split < width:
+                regroup_copy(nc.scalar.copy, grouped[:, split:width, :], raw[:, :, first + split : first + width])
             grouped_units[unit] = grouped
 
         def quantise(unit):
+            width = GROUPS[units[unit][0]][2] * P
             codes = codes_pool.tile([P, HALF], U32, name="codes", tag="codes", align_bytes=64)
             scales = codes_pool.tile([P, HALF], U8, name="scales", tag="scales", align_bytes=64)
             nc.vector.quantize_mx(
-                out=codes[:].bitcast(FP8X4),
-                scales=scales[:],
-                in_=grouped_units[unit][:].rearrange("q n t -> q (n t)"),
+                out=codes[:, 0:width].bitcast(FP8X4),
+                scales=scales[:, 0:width],
+                in_=grouped_units[unit][:, 0:width, :].rearrange("q n t -> q (n t)"),
             )
-            stationary_units[unit] = (codes, scales)
+            stationary[units[unit]] = (codes, scales)
 
-        def multiply(unit):
-            half, k_pass = units[unit]
-            codes, scales = stationary_units[unit]
-            for j in range(HALF_TILES):
-                if k_pass == 0:
-                    accumulators[(half, j)] = banks.tile([P, BATCH], F32, name="bank", tag="bank")
-                columns = slice(j * P, (j + 1) * P)
-                nc.tensor.matmul_mx(
-                    out=accumulators[(half, j)][:],
-                    lhsT=codes[:, columns].bitcast(FP8X4),
-                    lhsT_scale=scales[:, columns],
-                    rhs=moving_codes[:, k_pass, :].bitcast(FP8X4),
-                    rhs_scale=moving_scales[:, k_pass, :],
-                    start=(k_pass == 0),
-                    stop=(k_pass == PASSES - 1),
-                )
+        def multiply(group, j, k_pass):
+            codes, scales = stationary[(group, k_pass)]
+            if k_pass == 0:
+                accumulators[(group, j)] = sum_banks.tile([P, BATCH], F32, name="sums", tag="sums")
+            columns = slice(j * P, (j + 1) * P)
+            nc.tensor.matmul_mx(
+                out=accumulators[(group, j)][:],
+                lhsT=codes[:, columns].bitcast(FP8X4),
+                lhsT_scale=scales[:, columns],
+                rhs=moving_codes[:, k_pass, :].bitcast(FP8X4),
+                rhs_scale=moving_scales[:, k_pass, :],
+                start=(k_pass == 0),
+                stop=(k_pass == PASSES - 1),
+            )
 
-        def activate(half, j):
-            gate = half // 2
-            tile_index = (half % 2) * HALF_TILES + j
+        ALL = slice(0, BATCH_TILES)
+
+        def activate(group, j, b=ALL):
+            gate, first_tile, tiles = GROUPS[group]
+            tile_index = first_tile + j
+            rows = slice(b.start * P, b.stop * P)
             if gate == GATE_I:
-                result = i_gate[:, tile_index, :]
+                result = i_gate[:, tile_index, rows]
             else:
-                gate_tiles[(half, j)] = gate_pool.tile([P, BATCH], F32, name="gate_tile", tag="gate_tile")
-                result = gate_tiles[(half, j)][:]
-            bias_index = gate * (DIM // P) + tile_index
+                if b.start == 0:
+                    gate_tiles[(group, j)] = gate_pool.tile([P, BATCH], F32, name="gate_tile", tag="gate_tile")
+                result = gate_tiles[(group, j)][:, rows]
+            bias_index = gate * TILES + tile_index
             nc.scalar.activation(
                 out=result,
-                in_=accumulators[(half, j)][:],
+                in_=accumulators[(group, j)][:, rows],
                 func=gate_functions[gate],
                 bias=bias_columns[:, bias_index : bias_index + 1],
                 scale=1.0,
             )
 
-        def multiply_by_i(half, j):
-            g_tile = gate_tiles[(half, j)]
-            nc.vector.tensor_mul(out=g_tile[:], in0=g_tile[:], in1=i_gate[:, (half % 2) * HALF_TILES + j, :])
+        def multiply_by_i(group, j):
+            g_tile = gate_tiles[(group, j)]
+            tile_index = GROUPS[group][1] + j
+            nc.vector.tensor_mul(out=g_tile[:], in0=g_tile[:], in1=i_gate[:, tile_index, :])
 
-        def turn(half, j):
-            bank = banks.tile([P, BATCH_TILES, P], F32, name="bank", tag="bank")
-            for b in range(BATCH_TILES):
+        def turn(group, j, b=ALL):
+            bank = turn_banks.tile([P, BATCH_TILES, P], F32, name="turned", tag="turned")
+            for b_tile in range(b.start, b.stop):
                 nc.tensor.transpose(
-                    out=bank[:, b, :],
-                    in_=gate_tiles[(half, j)][:, b * P : (b + 1) * P],
+                    out=bank[:, b_tile, :],
+                    in_=gate_tiles[(group, j)][:, b_tile * P : (b_tile + 1) * P],
                     identity=identity[:],
                 )
-            turned_banks[(half, j)] = bank
+            turned_banks[(group, j)] = bank
 
-        def first_column(half, j):
-            return (half % 2) * HALF + j * P
+        def tile_columns(group, j):
+            first = (GROUPS[group][1] + j) * P
+            return slice(first, first + P)
 
-        def combine(half, j):
-            gate = half // 2
-            first = first_column(half, j)
-            columns = slice(first, first + P)
-            turned = turned_banks[(half, j)][:]
+        def tile_of_pair(pairs, group, j, b=ALL):
+            pair, odd = divmod(GROUPS[group][1] + j, 2)
+            return pairs[:, pair, b, odd * P : (odd + 1) * P]
+
+        def combine(group, j, b=ALL):
+            gate = GROUPS[group][0]
+            turned = turned_banks[(group, j)][:, b, :]
+            c_part = tile_of_pair(c_new, group, j, b)
+            h_part = tile_of_pair(h_new, group, j, b)
             if gate == GATE_F:
-                nc.vector.tensor_mul(out=c_new[:, :, columns], in0=turned, in1=c_rows[:, :, columns])
+                nc.vector.tensor_mul(out=c_part, in0=turned, in1=c_rows[:, b, tile_columns(group, j)])
             if gate == GATE_G:
-                nc.vector.tensor_add(out=c_new[:, :, columns], in0=turned, in1=c_new[:, :, columns])
+                nc.vector.tensor_add(out=c_part, in0=turned, in1=c_part)
             if gate == GATE_O:
-                nc.vector.tensor_mul(out=h_new[:, :, columns], in0=turned, in1=h_new[:, :, columns])
-            if j % STORE_TILES == STORE_TILES - 1:
-                piece = slice(first + P - STORE_TILES * P, first + P)
-                if gate == GATE_G:
-                    nc.sync.dma_start(out=c_new_rows[:, :, piece], in_=c_new[:, :, piece])
-                if gate == GATE_O:
-                    nc.sync.dma_start(out=h_new_rows[:, :, piece], in_=h_new[:, :, piece])
+                nc.vector.tensor_mul(out=h_part, in0=turned, in1=h_part)
 
-        def tanh_of_c_new(half, j):
-            first = first_column(half, j)
-            columns = slice(first, first + P)
-            nc.scalar.activation(out=h_new[:, :, columns], in_=c_new[:, :, columns], func=ACT.Tanh)
-
-        def finish(half, j, step):
-            gate = half // 2
-            if step == 0:
-                activate(half, j)
+        def store(group, j, b=ALL):
+            gate = GROUPS[group][0]
+            pair = (GROUPS[group][1] + j) // 2
+            piece = slice(pair * 2 * P, (pair + 1) * 2 * P)
             if gate == GATE_G:
-                if step == 1:
-                    multiply_by_i(half, j)
-                if step == 2:
-                    turn(half, j)
-                    combine(half, j)
-                if step == 3:
-                    tanh_of_c_new(half, j)
-            if gate in (GATE_F, GATE_O) and step == 1:
-                turn(half, j)
-                combine(half, j)
+                nc.sync.dma_start(out=c_new_rows[:, b, piece], in_=c_new[:, pair, b, :])
+            if gate == GATE_O:
+                nc.sync.dma_start(out=h_new_rows[:, b, piece], in_=h_new[:, pair, b, :])
+
+        def tanh_of_c_new(group, j):
+            nc.scalar.activation(
+                out=tile_of_pair(h_new, group, j), in_=tile_of_pair(c_new, group, j), func=ACT.Tanh
+            )
 
         def prepare_biases():
             nc.vector.tensor_add(out=bias_row_sums[:], in0=bias_rows[:, 0, :], in1=bias_rows[:, 1, :])
-            bias_bank = banks.tile([P, P], F32, name="bank", tag="bank")
+            bias_bank = turn_banks.tile([P, P], F32, name="turned", tag="turned")
             nc.tensor.transpose(out=bias_bank[:], in_=bias_row_sums[:], identity=identity[:])
-            nc.vector.tensor_copy(out=bias_columns[:], in_=bias_bank[:, 0 : GATES * DIM // P])
+            nc.vector.tensor_copy(out=bias_columns[:], in_=bias_bank[:, 0 : GATES * TILES])
 
-        def pipeline_round(r):
-            if r < UNITS:
-                regroup(r)
-                half, k_pass = units[r]
-                next_chunk = RAW_BUFFERS + (half // 2) * PASSES + k_pass
-                if half % 2 == 1 and next_chunk < CHUNKS:
-                    load_chunk(next_chunk)
-            if 1 <= r <= UNITS:
+        def pipeline_round(r, extra=0):
+            if r < len(units):
+                group, k_pass = units[r]
+                gate, first_tile, tiles = GROUPS[group]
+                width = tiles * P
+                split = VECTOR_SHARE[group] * width // 512 // 8 * 8
+                regroup(r, max(0, min(width, split + extra)))
+                if gate == GATE_G and first_tile + tiles == TILES and k_pass == 0:
+                    load_chunk(GATES * PASSES - 1)
+            for group, j in steps_in.get((r, "combine"), []):
+                if COMBINE_FIRST:
+                    combine_and_store(group, j)
+            if 1 <= r <= len(units):
                 quantise(r - 1)
-            for half in range(HALVES):
-                for j in range(HALF_TILES):
-                    finish(half, j, r - (last_unit[half] + 3 + j))
-            if 2 <= r <= UNITS + 1:
-                multiply(r - 2)
+            for group, j in steps_in.get((r, "act"), []):
+                activate(group, j)
+            for group, j in steps_in.get((r, "times_i"), []):
+                multiply_by_i(group, j)
+            for group, j in steps_in.get((r, "turn"), []):
+                turn(group, j)
+            for group, j in steps_in.get((r, "combine"), []):
+                if not COMBINE_FIRST:
+                    combine_and_store(group, j)
+            for group, j in steps_in.get((r, "tanh"), []):
+                tanh_of_c_new(group, j)
+            for group, j, k_pass in steps_in.get((r, "pass"), []):
+                multiply(group, j, k_pass)
+
+        def combine_and_store(group, j):
+            combine(group, j)
+            if (GROUPS[group][1] + j) % STORE_TILES == STORE_TILES - 1:
+                store(group, j)
+
+        def last_tiles():
+            group = len(GROUPS) - 1
+            tiles = GROUPS[group][2]
+            halves = [slice(0, 2), slice(2, 4)]
+            for b in halves:
+                for j in range(tiles):
+                    activate(group, j, b)
+            for b in halves:
+                for j in range(tiles):
+                    turn(group, j, b)
+                    combine(group, j, b)
+                store(group, tiles - 1, b)
 
         with tc.manual_schedule():
             make_identity(nc, identity[:])
             nc.vector.memset(table_warmer[:], 0.0)
             nc.scalar.activation(out=table_warmer[:], in_=table_warmer[:], func=ACT.Sigmoid)
+            nc.vector.memset(bias_rows[:], 0.0)
             x_rows = raw_pool.tile([P, BATCH_TILES, DIM], BF16, name="raw", tag="raw")
             h_rows = raw_pool.tile([P, BATCH_TILES, DIM], BF16, name="raw", tag="raw")
-            load_batch_rows(x_rows, x)
-            nc.vector.memset(bias_rows[:], 0.0)
-            for gate in range(GATES):
-                for source in range(2):
-                    nc.scalar.dma_start(
-                        out=bias_rows[gate * (DIM // P) : (gate + 1) * (DIM // P), source, :],
-                        in_=gate_biases[gate][source].rearrange("(d p) -> d p", p=P),
-                    )
-            load_batch_rows(h_rows, h)
-            for chunk in range(2 * PASSES):
-                load_chunk(chunk)
-            load_batch_rows(c_rows, c)
-            for chunk in range(2 * PASSES, RAW_BUFFERS - 2):
-                load_chunk(chunk)
-            quantise_moving(0, x_rows)
-            quantise_moving(1, h_rows)
-            for chunk in range(RAW_BUFFERS - 2, RAW_BUFFERS):
-                load_chunk(chunk)
-            for r in range(HEAD_ROUNDS):
+            load_half_chunk(0, 0)
+            load_batch_rows(x_rows, x, 0)
+            load_bias(0)
+            load_batch_rows(x_rows, x, 2)
+            load_bias(1)
+            load_half_chunk(0, 1)
+            load_bias(2)
+            load_chunk(1)
+            load_bias(3)
+            load_batch_rows(h_rows, h, 0)
+            load_bias(4)
+            load_batch_rows(h_rows, h, 2)
+            load_bias(5)
+            load_chunk(2)
+            load_bias(6)
+            load_chunk(3)
+            load_bias(7)
+            for half in range(2):
+                for chunk in range(PASSES, 2 * PASSES):
+                    load_half_chunk(chunk, half)
+                if half == 0:
+                    load_batch_rows(c_rows, c, 0)
+                    load_batch_rows(c_rows, c, 2)
+            pipeline_round(0, -176)
+            x_grouped = [grouped_tile(), grouped_tile()]
+            turn_moving(x_rows, x_grouped, 0)
+            turn_moving(x_rows, x_grouped, 1)
+            pipeline_round(1)
+            quantise_moving(0, x_grouped)
+            pipeline_round(2, -88)
+            h_grouped = [grouped_tile(), grouped_tile()]
+            pipeline_round(3)
+            turn_moving(h_rows, h_grouped, 0)
+            turn_moving(h_rows, h_grouped, 1)
+            pipeline_round(4, -88)
+            quantise_moving(1, h_grouped)
+            for r in range(5, 8):
                 pipeline_round(r)
             prepare_biases()
-            for r in range(HEAD_ROUNDS, UNITS + 3 + HALF_TILES + FINISH_STEPS):
+            for chunk in range(2 * PASSES, GATES * PASSES - 1):
+                load_chunk(chunk)
+            for r in range(8, len(units) + EXTRA_ROUNDS):
                 pipeline_round(r)
+            last_tiles()

@@ -36,10 +36,11 @@ GROUPS = [
 RAW_BUFFERS = 7
 RAW_HALF_BUFFERS = 10
 STORE_TILES = 2
-PASS_BY_PASS = (0, 7, 8,)
-LAGS = [(2, 1, 1, 0), (2, 1, 1, 0), (2, 1, 1, 0), (2, 1, 1, 0), (2, 1, 1, 0), (2, 1, 1, 0), (2, 1, 1, 0), (2, 1, 1, 0), (2, 1, 1, 0)]
+PASS_BY_PASS = (0, 6, 7, 8,)
+PAIRS = (4, 5,)
+LAGS = [(2, 1, 1, 0), (2, 1, 1, 0), (2, 1, 1, 0), (2, 1, 1, 0), (2, 1, 1, 0), (2, 1, 1, 0), (2, 1, 1, 0), (2, 1, 1, 0), (1, 1, 1, 0)]
 ACT_SPACING = [1, 2, 2, 2, 2, 2, 2, 2, 2]
-VECTOR_SHARE = [256, 328, 256, 256, 256, 256, 256, 256, 256]
+VECTOR_SHARE = [256, 328, 328, 300, 256, 240, 240, 240, 240]
 COMBINE_FIRST = False
 EXTRA_ROUNDS = 4
 
@@ -58,8 +59,8 @@ def tile_lstmcell_kernel(
     gate_weights = [(wxi, whi), (wxf, whf), (wxg, whg), (wxo, who)]
     gate_biases = [(bxi, bhi), (bxf, bhf), (bxg, bhg), (bxo, bho)]
     gate_functions = [ACT.Sigmoid, ACT.Sigmoid, ACT.Tanh, ACT.Sigmoid]
-    h_new_rows = out_0.rearrange("(b p) n -> p b n", p=P)
-    c_new_rows = out_1.rearrange("(b p) n -> p b n", p=P)
+    h_new_rows = out_0.rearrange("(p b) n -> p b n", p=P)
+    c_new_rows = out_1.rearrange("(p b) n -> p b n", p=P)
 
     with ExitStack() as stack:
         keep = stack.enter_context(tc.tile_pool(name="keep", bufs=1))
@@ -68,8 +69,7 @@ def tile_lstmcell_kernel(
         grouped_pool = stack.enter_context(tc.tile_pool(name="grouped", bufs=5))
         codes_pool = stack.enter_context(tc.tile_pool(name="codes", bufs=9))
         gate_pool = stack.enter_context(tc.tile_pool(name="gate", bufs=7))
-        sum_banks = stack.enter_context(tc.psum_pool(name="sums", bufs=5))
-        turn_banks = stack.enter_context(tc.psum_pool(name="turns", bufs=3))
+        banks = stack.enter_context(tc.psum_pool(name="banks", bufs=1))
 
         identity = keep.tile([P, P], F32)
         table_warmer = keep.tile([P, 1], F32)
@@ -99,6 +99,7 @@ def tile_lstmcell_kernel(
             gate, first_tile, tiles = GROUPS[group]
             pass_lag, act_lag, turn_lag, combine_lag = LAGS[group]
             last = units.index((group, PASSES - 1))
+            turned_at = {}
             for j in range(tiles):
                 for k_pass in range(PASSES):
                     if group in PASS_BY_PASS:
@@ -113,10 +114,24 @@ def tile_lstmcell_kernel(
                     plan(r + 1, "times_i", (group, j))
                     r = r + 1
                 if gate != GATE_I:
-                    plan(r + turn_lag, "turn", (group, j))
-                    plan(r + turn_lag + combine_lag, "combine", (group, j))
+                    turned_at[j] = r + turn_lag
+            for j in turned_at:
+                r = turned_at[j | 1] if group in PAIRS else turned_at[j]
+                plan(r, "turn", (group, j))
+                r = r + combine_lag + (j & 1 if group in PAIRS else 0)
+                plan(r, "combine", (group, j))
                 if gate == GATE_G:
-                    plan(r + turn_lag + combine_lag + 1, "tanh", (group, j))
+                    plan(r + 1, "tanh", (group, j))
+
+        free_banks = list(range(8))
+        bank_of = {}
+
+        def take_bank(shape, key):
+            bank_of[key] = free_banks.pop(0)
+            return banks.tile(shape, F32, name="bank%d" % bank_of[key], tag="bank%d" % bank_of[key])
+
+        def give_back(key):
+            free_banks.append(bank_of[key])
 
         raw_chunks = {}
         grouped_units = {}
@@ -126,7 +141,7 @@ def tile_lstmcell_kernel(
         turned_banks = {}
 
         def load_batch_rows(rows, source, first):
-            view = source.rearrange("(b p) k -> p b k", p=P)
+            view = source.rearrange("(p b) k -> p b k", p=P)
             nc.sync.dma_start(out=rows[:, first : first + 2, :], in_=view[:, first : first + 2, :])
 
         def chunk_rows(chunk):
@@ -156,7 +171,7 @@ def tile_lstmcell_kernel(
         def turn_moving(rows, grouped, side):
             words = rows[:].bitcast(F32)
             for g in range(2):
-                bank = turn_banks.tile([P, 2, 2 * P], F32, name="turned", tag="turned")
+                bank = take_bank([P, 2, 2 * P], "moving")
                 for u in range(2):
                     for b in range(2):
                         first_word = (K_PASS // 2) * g + u
@@ -170,6 +185,7 @@ def tile_lstmcell_kernel(
                     out=grouped[g][:].bitcast(F32)[:, side * 2 * P : (side + 1) * 2 * P, :],
                     in_=bank[:].rearrange("q u b -> q b u"),
                 )
+                give_back("moving")
 
         def quantise_moving(operand, grouped):
             for g in range(2):
@@ -216,7 +232,7 @@ def tile_lstmcell_kernel(
         def multiply(group, j, k_pass):
             codes, scales = stationary[(group, k_pass)]
             if k_pass == 0:
-                accumulators[(group, j)] = sum_banks.tile([P, BATCH], F32, name="sums", tag="sums")
+                accumulators[(group, j)] = take_bank([P, BATCH], ("sums", group, j))
             columns = slice(j * P, (j + 1) * P)
             nc.tensor.matmul_mx(
                 out=accumulators[(group, j)][:],
@@ -248,6 +264,8 @@ def tile_lstmcell_kernel(
                 bias=bias_columns[:, bias_index : bias_index + 1],
                 scale=1.0,
             )
+            if b.stop == BATCH_TILES:
+                give_back(("sums", group, j))
 
         def multiply_by_i(group, j):
             g_tile = gate_tiles[(group, j)]
@@ -255,7 +273,7 @@ def tile_lstmcell_kernel(
             nc.vector.tensor_mul(out=g_tile[:], in0=g_tile[:], in1=i_gate[:, tile_index, :])
 
         def turn(group, j, b=ALL):
-            bank = turn_banks.tile([P, BATCH_TILES, P], F32, name="turned", tag="turned")
+            bank = take_bank([P, BATCH_TILES, P], ("turned", group, j))
             for b_tile in range(b.start, b.stop):
                 nc.tensor.transpose(
                     out=bank[:, b_tile, :],
@@ -283,6 +301,7 @@ def tile_lstmcell_kernel(
                 nc.vector.tensor_add(out=c_part, in0=turned, in1=c_part)
             if gate == GATE_O:
                 nc.vector.tensor_mul(out=h_part, in0=turned, in1=h_part)
+            give_back(("turned", group, j))
 
         def store(group, j, b=ALL):
             gate = GROUPS[group][0]
@@ -300,9 +319,10 @@ def tile_lstmcell_kernel(
 
         def prepare_biases():
             nc.vector.tensor_add(out=bias_row_sums[:], in0=bias_rows[:, 0, :], in1=bias_rows[:, 1, :])
-            bias_bank = turn_banks.tile([P, P], F32, name="turned", tag="turned")
+            bias_bank = take_bank([P, P], "bias")
             nc.tensor.transpose(out=bias_bank[:], in_=bias_row_sums[:], identity=identity[:])
             nc.vector.tensor_copy(out=bias_columns[:], in_=bias_bank[:, 0 : GATES * TILES])
+            give_back("bias")
 
         def pipeline_round(r, extra=0):
             if r < len(units):

@@ -40,7 +40,7 @@ PASS_BY_PASS = (0, 6, 7, 8,)
 PAIRS = (4, 5,)
 LAGS = [(2, 1, 1, 0), (2, 1, 1, 0), (2, 1, 1, 0), (2, 1, 1, 0), (2, 1, 1, 0), (2, 1, 1, 0), (2, 1, 1, 0), (2, 1, 1, 0), (1, 1, 1, 0)]
 ACT_SPACING = [1, 2, 2, 2, 2, 2, 2, 2, 2]
-VECTOR_SHARE = [256, 328, 328, 300, 256, 240, 240, 240, 240]
+VECTOR_SHARE = [256, 320, 320, 304, 256, 240, 240, 240, 240]
 COMBINE_FIRST = False
 EXTRA_ROUNDS = 4
 
@@ -201,8 +201,8 @@ def tile_lstmcell_kernel(
 
         def regroup_copy(copy, grouped_part, raw_part):
             copy(
-                out=grouped_part.rearrange("q (n i) t -> q n t i", i=4),
-                in_=raw_part.rearrange("q t (n i) -> q n t i", i=4),
+                out=grouped_part.rearrange("q (n i) t -> q n t i", i=8),
+                in_=raw_part.rearrange("q t (n i) -> q n t i", i=8),
             )
 
         def regroup(unit, split):
@@ -329,7 +329,7 @@ def tile_lstmcell_kernel(
                 group, k_pass = units[r]
                 gate, first_tile, tiles = GROUPS[group]
                 width = tiles * P
-                split = VECTOR_SHARE[group] * width // 512 // 8 * 8
+                split = VECTOR_SHARE[group] * width // 512 // 16 * 16
                 regroup(r, max(0, min(width, split + extra)))
                 if gate == GATE_G and first_tile + tiles == TILES and k_pass == 0:
                     load_chunk(GATES * PASSES - 1)
@@ -406,12 +406,12 @@ def tile_lstmcell_kernel(
             turn_moving(x_rows, x_grouped, 1)
             pipeline_round(1)
             quantise_moving(0, x_grouped)
-            pipeline_round(2, -88)
+            pipeline_round(2, -80)
             h_grouped = [grouped_tile(), grouped_tile()]
             pipeline_round(3)
             turn_moving(h_rows, h_grouped, 0)
             turn_moving(h_rows, h_grouped, 1)
-            pipeline_round(4, -88)
+            pipeline_round(4, -80)
             quantise_moving(1, h_grouped)
             for r in range(5, 8):
                 pipeline_round(r)

@@ -33,16 +33,16 @@ GROUPS = [
     (GATE_O, 4, 2),
     (GATE_O, 6, 2),
 ]
-RAW_BUFFERS = 7
-RAW_HALF_BUFFERS = 10
+RAW_BUFFERS = 11
+RAW_HALF_BUFFERS = 2
 STORE_TILES = 2
-PASS_BY_PASS = (0, 6, 7, 8,)
+PASS_BY_PASS = (0, 2, 6, 7, 8,)
 PAIRS = (4, 5,)
-LAGS = [(2, 1, 1, 0), (2, 1, 1, 0), (2, 1, 1, 0), (2, 1, 1, 0), (2, 1, 1, 0), (2, 1, 1, 0), (2, 1, 1, 0), (2, 1, 1, 0), (1, 1, 1, 0)]
-ACT_SPACING = [1, 2, 2, 2, 2, 2, 2, 2, 2]
-VECTOR_SHARE = [256, 320, 320, 304, 256, 240, 240, 240, 240]
+LAGS = [(2, 1, 1, 0), (2, 1, 1, 0), (2, 1, 1, 0), (2, 1, 1, 0), (2, 1, 1, 0), (2, 1, 1, 0), (2, 1, 1, 1), (2, 1, 1, 1), (1, 1, 1, 0)]
+ACT_SPACING = [1, 2, 1, 2, 2, 2, 2, 2, 2]
+VECTOR_SHARE = [256, 320, 320, 304, 256, 240, 240, 240, 320]
 COMBINE_FIRST = False
-EXTRA_ROUNDS = 4
+EXTRA_ROUNDS = 5
 
 FLOPS = 2 * BATCH * 2 * DIM * GATES * DIM
 
@@ -83,12 +83,7 @@ def tile_lstmcell_kernel(
         c_new = keep.tile([P, TILES // 2, BATCH_TILES, 2 * P], F32)
         h_new = keep.tile([P, TILES // 2, BATCH_TILES, 2 * P], F32)
 
-        units = []
-        for k_pass in range(PASSES):
-            units += [(0, k_pass), (1, k_pass)]
-        for group in range(2, len(GROUPS)):
-            for k_pass in range(PASSES):
-                units.append((group, k_pass))
+        units = [(0, 0), (1, 0), (0, 1), (1, 1), (0, 2), (1, 2), (0, 3), (1, 3), (2, 0), (3, 0), (2, 1), (3, 1), (2, 2), (3, 2), (2, 3), (3, 3), (4, 0), (4, 1), (4, 2), (4, 3), (5, 0), (5, 1), (5, 2), (5, 3), (6, 0), (6, 1), (6, 2), (6, 3), (7, 0), (7, 1), (7, 2), (7, 3), (8, 0), (8, 1), (8, 2), (8, 3)]
 
         steps_in = {}
 
@@ -394,12 +389,10 @@ def tile_lstmcell_kernel(
             load_bias(6)
             load_chunk(3)
             load_bias(7)
-            for half in range(2):
-                for chunk in range(PASSES, 2 * PASSES):
-                    load_half_chunk(chunk, half)
-                if half == 0:
-                    load_batch_rows(c_rows, c, 0)
-                    load_batch_rows(c_rows, c, 2)
+            for chunk in range(PASSES, 2 * PASSES):
+                load_chunk(chunk)
+            load_batch_rows(c_rows, c, 0)
+            load_batch_rows(c_rows, c, 2)
             pipeline_round(0, -176)
             x_grouped = [grouped_tile(), grouped_tile()]
             turn_moving(x_rows, x_grouped, 0)

@@ -33,8 +33,7 @@ GROUPS = [
     (GATE_O, 4, 2),
     (GATE_O, 6, 2),
 ]
-RAW_BUFFERS = 11
-RAW_HALF_BUFFERS = 2
+RAW_BUFFERS = 12
 STORE_TILES = 2
 PASS_BY_PASS = (0, 2, 6, 7, 8,)
 PAIRS = (4, 5,)
@@ -65,7 +64,6 @@ def tile_lstmcell_kernel(
     with ExitStack() as stack:
         keep = stack.enter_context(tc.tile_pool(name="keep", bufs=1))
         raw_pool = stack.enter_context(tc.tile_pool(name="raw", bufs=RAW_BUFFERS))
-        raw_half_pool = stack.enter_context(tc.tile_pool(name="raw_half", bufs=RAW_HALF_BUFFERS))
         grouped_pool = stack.enter_context(tc.tile_pool(name="grouped", bufs=5))
         codes_pool = stack.enter_context(tc.tile_pool(name="codes", bufs=9))
         gate_pool = stack.enter_context(tc.tile_pool(name="gate", bufs=7))
@@ -150,11 +148,6 @@ def tile_lstmcell_kernel(
             nc.sync.dma_start(out=raw[:], in_=chunk_rows(chunk))
             raw_chunks[(chunk, 0)] = raw[:, :, 0:HALF]
             raw_chunks[(chunk, 1)] = raw[:, :, HALF:DIM]
-
-        def load_half_chunk(chunk, half):
-            raw = raw_half_pool.tile([P, PACK, HALF], BF16, name="raw_half", tag="raw_half")
-            nc.sync.dma_start(out=raw[:], in_=chunk_rows(chunk)[:, :, half * HALF : (half + 1) * HALF])
-            raw_chunks[(chunk, half)] = raw[:]
 
         def load_bias(index):
             gate, source = divmod(index, 2)
@@ -312,10 +305,15 @@ def tile_lstmcell_kernel(
                 out=tile_of_pair(h_new, group, j), in_=tile_of_pair(c_new, group, j), func=ACT.Tanh
             )
 
-        def prepare_biases():
+        def sum_biases():
             nc.vector.tensor_add(out=bias_row_sums[:], in0=bias_rows[:, 0, :], in1=bias_rows[:, 1, :])
+
+        def turn_biases():
             bias_bank = take_bank([P, P], "bias")
             nc.tensor.transpose(out=bias_bank[:], in_=bias_row_sums[:], identity=identity[:])
+            return bias_bank
+
+        def keep_biases(bias_bank):
             nc.vector.tensor_copy(out=bias_columns[:], in_=bias_bank[:, 0 : GATES * TILES])
             give_back("bias")
 
@@ -372,12 +370,11 @@ def tile_lstmcell_kernel(
             nc.vector.memset(bias_rows[:], 0.0)
             x_rows = raw_pool.tile([P, BATCH_TILES, DIM], BF16, name="raw", tag="raw")
             h_rows = raw_pool.tile([P, BATCH_TILES, DIM], BF16, name="raw", tag="raw")
-            load_half_chunk(0, 0)
             load_batch_rows(x_rows, x, 0)
             load_bias(0)
             load_batch_rows(x_rows, x, 2)
             load_bias(1)
-            load_half_chunk(0, 1)
+            load_chunk(0)
             load_bias(2)
             load_chunk(1)
             load_bias(3)
@@ -393,12 +390,12 @@ def tile_lstmcell_kernel(
                 load_chunk(chunk)
             load_batch_rows(c_rows, c, 0)
             load_batch_rows(c_rows, c, 2)
-            pipeline_round(0, -176)
             x_grouped = [grouped_tile(), grouped_tile()]
             turn_moving(x_rows, x_grouped, 0)
             turn_moving(x_rows, x_grouped, 1)
-            pipeline_round(1)
             quantise_moving(0, x_grouped)
+            pipeline_round(0)
+            pipeline_round(1)
             pipeline_round(2, -80)
             h_grouped = [grouped_tile(), grouped_tile()]
             pipeline_round(3)
@@ -408,7 +405,11 @@ def tile_lstmcell_kernel(
             quantise_moving(1, h_grouped)
             for r in range(5, 8):
                 pipeline_round(r)
-            prepare_biases()
+                if r == 5:
+                    sum_biases()
+                if r == 6:
+                    bias_bank = turn_biases()
+            keep_biases(bias_bank)
             for chunk in range(2 * PASSES, GATES * PASSES - 1):
                 load_chunk(chunk)
             for r in range(8, len(units) + EXTRA_ROUNDS):

@@ -33,13 +33,14 @@ GROUPS = [
     (GATE_O, 4, 2),
     (GATE_O, 6, 2),
 ]
-RAW_BUFFERS = 12
+RAW_BUFFERS = 8
+RAW_HALF_BUFFERS = 8
 STORE_TILES = 2
 PASS_BY_PASS = (0, 2, 6, 7, 8,)
 PAIRS = (4, 5,)
 LAGS = [(2, 1, 1, 0), (2, 1, 1, 0), (2, 1, 1, 0), (2, 1, 1, 0), (2, 1, 1, 0), (2, 1, 1, 0), (2, 1, 1, 1), (2, 1, 1, 1), (1, 1, 1, 0)]
 ACT_SPACING = [1, 2, 1, 2, 2, 2, 2, 2, 2]
-VECTOR_SHARE = [256, 320, 320, 304, 256, 240, 240, 240, 320]
+VECTOR_SHARE = [256, 320, 320, 304, 272, 256, 256, 240, 320]
 COMBINE_FIRST = False
 EXTRA_ROUNDS = 5
 
@@ -64,6 +65,7 @@ def tile_lstmcell_kernel(
     with ExitStack() as stack:
         keep = stack.enter_context(tc.tile_pool(name="keep", bufs=1))
         raw_pool = stack.enter_context(tc.tile_pool(name="raw", bufs=RAW_BUFFERS))
+        raw_half_pool = stack.enter_context(tc.tile_pool(name="raw_half", bufs=RAW_HALF_BUFFERS))
         grouped_pool = stack.enter_context(tc.tile_pool(name="grouped", bufs=5))
         codes_pool = stack.enter_context(tc.tile_pool(name="codes", bufs=9))
         gate_pool = stack.enter_context(tc.tile_pool(name="gate", bufs=7))
@@ -148,6 +150,11 @@ def tile_lstmcell_kernel(
             nc.sync.dma_start(out=raw[:], in_=chunk_rows(chunk))
             raw_chunks[(chunk, 0)] = raw[:, :, 0:HALF]
             raw_chunks[(chunk, 1)] = raw[:, :, HALF:DIM]
+
+        def load_half_chunk(chunk, half):
+            raw = raw_half_pool.tile([P, PACK, HALF], BF16, name="raw_half", tag="raw_half")
+            nc.sync.dma_start(out=raw[:], in_=chunk_rows(chunk)[:, :, half * HALF : (half + 1) * HALF])
+            raw_chunks[(chunk, half)] = raw[:]
 
         def load_bias(index):
             gate, source = divmod(index, 2)
@@ -324,8 +331,6 @@ def tile_lstmcell_kernel(
                 width = tiles * P
                 split = VECTOR_SHARE[group] * width // 512 // 16 * 16
                 regroup(r, max(0, min(width, split + extra)))
-                if gate == GATE_G and first_tile + tiles == TILES and k_pass == 0:
-                    load_chunk(GATES * PASSES - 1)
             for group, j in steps_in.get((r, "combine"), []):
                 if COMBINE_FIRST:
                     combine_and_store(group, j)
@@ -386,14 +391,13 @@ def tile_lstmcell_kernel(
             load_bias(6)
             load_chunk(3)
             load_bias(7)
-            for chunk in range(PASSES, 2 * PASSES):
-                load_chunk(chunk)
-            load_batch_rows(c_rows, c, 0)
-            load_batch_rows(c_rows, c, 2)
+            load_chunk(4)
+            load_chunk(5)
             x_grouped = [grouped_tile(), grouped_tile()]
             turn_moving(x_rows, x_grouped, 0)
             turn_moving(x_rows, x_grouped, 1)
             quantise_moving(0, x_grouped)
+            load_chunk(6)
             pipeline_round(0)
             pipeline_round(1)
             pipeline_round(2, -80)
@@ -401,6 +405,12 @@ def tile_lstmcell_kernel(
             pipeline_round(3)
             turn_moving(h_rows, h_grouped, 0)
             turn_moving(h_rows, h_grouped, 1)
+            load_chunk(7)
+            load_batch_rows(c_rows, c, 0)
+            load_batch_rows(c_rows, c, 2)
+            for half in range(2):
+                for chunk in range(2 * PASSES, 3 * PASSES):
+                    load_half_chunk(chunk, half)
             pipeline_round(4, -80)
             quantise_moving(1, h_grouped)
             for r in range(5, 8):
@@ -410,7 +420,7 @@ def tile_lstmcell_kernel(
                 if r == 6:
                     bias_bank = turn_biases()
             keep_biases(bias_bank)
-            for chunk in range(2 * PASSES, GATES * PASSES - 1):
+            for chunk in range(3 * PASSES, GATES * PASSES):
                 load_chunk(chunk)
             for r in range(8, len(units) + EXTRA_ROUNDS):
                 pipeline_round(r)

@@ -40,7 +40,7 @@ PASS_BY_PASS = (0, 2, 6, 7, 8,)
 PAIRS = (4, 5,)
 LAGS = [(2, 1, 1, 0), (2, 1, 1, 0), (2, 1, 1, 0), (2, 1, 1, 0), (2, 1, 1, 0), (2, 1, 1, 0), (2, 1, 1, 1), (2, 1, 1, 1), (1, 1, 1, 0)]
 ACT_SPACING = [1, 2, 1, 2, 2, 2, 2, 2, 2]
-VECTOR_SHARE = [256, 320, 320, 304, 272, 256, 256, 240, 320]
+VECTOR_SHARE = [240, 304, 320, 320, 272, 240, 256, 240, 320]
 COMBINE_FIRST = False
 EXTRA_ROUNDS = 5
 
@@ -383,9 +383,8 @@ def tile_lstmcell_kernel(
             load_bias(2)
             load_chunk(1)
             load_bias(3)
-            load_batch_rows(h_rows, h, 0)
+            nc.sync.dma_start(out=h_rows[:], in_=h.rearrange("(p b) k -> p b k", p=P))
             load_bias(4)
-            load_batch_rows(h_rows, h, 2)
             load_bias(5)
             load_chunk(2)
             load_bias(6)

from contextlib import ExitStack

import concourse.mybir as mybir
from concourse.masks import make_identity

F32 = mybir.dt.float32
BF16 = mybir.dt.bfloat16
U32 = mybir.dt.uint32
U8 = mybir.dt.uint8
FP8X4 = mybir.dt.float8_e4m3fn_x4
ACT = mybir.ActivationFunctionType

P = 128
PACK = 4
K_PASS = P * PACK
BATCH = 512
DIM = 1024
BATCH_TILES = BATCH // P
PASSES = 2 * DIM // K_PASS
GATE_I, GATE_F, GATE_G, GATE_O = 0, 1, 2, 3
GATES = 4
TILES = DIM // P
HALF = DIM // 2

GROUPS = [
    (GATE_I, 0, 4),
    (GATE_I, 4, 4),
    (GATE_F, 0, 4),
    (GATE_F, 4, 4),
    (GATE_G, 0, 4),
    (GATE_G, 4, 4),
    (GATE_O, 0, 4),
    (GATE_O, 4, 2),
    (GATE_O, 6, 2),
]
RAW_BUFFERS = 8
RAW_HALF_BUFFERS = 8
STORE_TILES = 2
PASS_BY_PASS = (0, 2, 6, 7, 8,)
PAIRS = (4, 5,)
LAGS = [(2, 1, 1, 0), (2, 1, 1, 0), (2, 1, 1, 0), (2, 1, 1, 0), (2, 1, 1, 0), (2, 1, 1, 0), (2, 1, 1, 1), (2, 1, 1, 1), (1, 1, 1, 0)]
ACT_SPACING = [1, 2, 1, 2, 2, 2, 2, 2, 2]
VECTOR_SHARE = [240, 304, 320, 320, 272, 240, 256, 240, 320]
COMBINE_FIRST = False
EXTRA_ROUNDS = 5

FLOPS = 2 * BATCH * 2 * DIM * GATES * DIM


def tile_lstmcell_kernel(
    tc, x, h, c,
    wxi, whi, bxi, bhi,
    wxf, whf, bxf, bhf,
    wxg, whg, bxg, bhg,
    wxo, who, bxo, bho,
    out_0, out_1,
):
    nc = tc.nc
    gate_weights = [(wxi, whi), (wxf, whf), (wxg, whg), (wxo, who)]
    gate_biases = [(bxi, bhi), (bxf, bhf), (bxg, bhg), (bxo, bho)]
    gate_functions = [ACT.Sigmoid, ACT.Sigmoid, ACT.Tanh, ACT.Sigmoid]
    h_new_rows = out_0.rearrange("(p b) n -> p b n", p=P)
    c_new_rows = out_1.rearrange("(p b) n -> p b n", p=P)

    with ExitStack() as stack:
        keep = stack.enter_context(tc.tile_pool(name="keep", bufs=1))
        raw_pool = stack.enter_context(tc.tile_pool(name="raw", bufs=RAW_BUFFERS))
        raw_half_pool = stack.enter_context(tc.tile_pool(name="raw_half", bufs=RAW_HALF_BUFFERS))
        grouped_pool = stack.enter_context(tc.tile_pool(name="grouped", bufs=5))
        codes_pool = stack.enter_context(tc.tile_pool(name="codes", bufs=9))
        gate_pool = stack.enter_context(tc.tile_pool(name="gate", bufs=7))
        banks = stack.enter_context(tc.psum_pool(name="banks", bufs=1))

        identity = keep.tile([P, P], F32)
        table_warmer = keep.tile([P, 1], F32)
        bias_rows = keep.tile([P, 2, P], BF16)
        bias_row_sums = keep.tile([P, P], F32)
        bias_columns = keep.tile([P, GATES * TILES], F32)
        moving_codes = keep.tile([P, PASSES, BATCH], U32, align_bytes=64)
        moving_scales = keep.tile([P, PASSES, BATCH], U8, align_bytes=64)
        c_rows = keep.tile([P, BATCH_TILES, DIM], BF16)
        i_gate = keep.tile([P, TILES, BATCH], F32)
        c_new = keep.tile([P, TILES // 2, BATCH_TILES, 2 * P], F32)
        h_new = keep.tile([P, TILES // 2, BATCH_TILES, 2 * P], F32)

        units = [(0, 0), (1, 0), (0, 1), (1, 1), (0, 2), (1, 2), (0, 3), (1, 3), (2, 0), (3, 0), (2, 1), (3, 1), (2, 2), (3, 2), (2, 3), (3, 3), (4, 0), (4, 1), (4, 2), (4, 3), (5, 0), (5, 1), (5, 2), (5, 3), (6, 0), (6, 1), (6, 2), (6, 3), (7, 0), (7, 1), (7, 2), (7, 3), (8, 0), (8, 1), (8, 2), (8, 3)]

        steps_in = {}

        def plan(r, name, item):
            steps_in.setdefault((r, name), []).append(item)

        for group in range(len(GROUPS)):
            gate, first_tile, tiles = GROUPS[group]
            pass_lag, act_lag, turn_lag, combine_lag = LAGS[group]
            last = units.index((group, PASSES - 1))
            turned_at = {}
            for j in range(tiles):
                for k_pass in range(PASSES):
                    if group in PASS_BY_PASS:
                        plan(units.index((group, k_pass)) + pass_lag, "pass", (group, j, k_pass))
                    else:
                        plan(last + pass_lag + j, "pass", (group, j, k_pass))
                if group == len(GROUPS) - 1:
                    continue
                r = last + pass_lag + act_lag + ACT_SPACING[group] * j // 2
                plan(r, "act", (group, j))
                if gate == GATE_G:
                    plan(r + 1, "times_i", (group, j))
                    r = r + 1
                if gate != GATE_I:
                    turned_at[j] = r + turn_lag
            for j in turned_at:
                r = turned_at[j | 1] if group in PAIRS else turned_at[j]
                plan(r, "turn", (group, j))
                r = r + combine_lag + (j & 1 if group in PAIRS else 0)
                plan(r, "combine", (group, j))
                if gate == GATE_G:
                    plan(r + 1, "tanh", (group, j))

        free_banks = list(range(8))
        bank_of = {}

        def take_bank(shape, key):
            bank_of[key] = free_banks.pop(0)
            return banks.tile(shape, F32, name="bank%d" % bank_of[key], tag="bank%d" % bank_of[key])

        def give_back(key):
            free_banks.append(bank_of[key])

        raw_chunks = {}
        grouped_units = {}
        stationary = {}
        accumulators = {}
        gate_tiles = {}
        turned_banks = {}

        def load_batch_rows(rows, source, first):
            view = source.rearrange("(p b) k -> p b k", p=P)
            nc.sync.dma_start(out=rows[:, first : first + 2, :], in_=view[:, first : first + 2, :])

        def chunk_rows(chunk):
            gate, k_pass = divmod(chunk, PASSES)
            first_row = (k_pass % 2) * K_PASS
            weight = gate_weights[gate][k_pass // 2]
            return weight[first_row : first_row + K_PASS, :].rearrange("(q t) n -> q t n", t=PACK)

        def load_chunk(chunk):
            raw = raw_pool.tile([P, PACK, DIM], BF16, name="raw", tag="raw")
            nc.sync.dma_start(out=raw[:], in_=chunk_rows(chunk))
            raw_chunks[(chunk, 0)] = raw[:, :, 0:HALF]
            raw_chunks[(chunk, 1)] = raw[:, :, HALF:DIM]

        def load_half_chunk(chunk, half):
            raw = raw_half_pool.tile([P, PACK, HALF], BF16, name="raw_half", tag="raw_half")
            nc.sync.dma_start(out=raw[:], in_=chunk_rows(chunk)[:, :, half * HALF : (half + 1) * HALF])
            raw_chunks[(chunk, half)] = raw[:]

        def load_bias(index):
            gate, source = divmod(index, 2)
            nc.sync.dma_start(
                out=bias_rows[gate * TILES : (gate + 1) * TILES, source, :],
                in_=gate_biases[gate][source].rearrange("(d p) -> d p", p=P),
            )

        def turn_moving(rows, grouped, side):
            words = rows[:].bitcast(F32)
            for g in range(2):
                bank = take_bank([P, 2, 2 * P], "moving")
                for u in range(2):
                    for b in range(2):
                        first_word = (K_PASS // 2) * g + u
                        nc.tensor.transpose(
                            out=bank[:, u, b * P : (b + 1) * P],
                            in_=words[:, 2 * side + b, first_word : first_word + 2 * P - 1 : 2],
                            identity=identity[:],
                        )
                copy = nc.vector.tensor_copy if side == 0 else nc.scalar.copy
                copy(
                    out=grouped[g][:].bitcast(F32)[:, side * 2 * P : (side + 1) * 2 * P, :],
                    in_=bank[:].rearrange("q u b -> q b u"),
                )
                give_back("moving")

        def quantise_moving(operand, grouped):
            for g in range(2):
                k_pass = 2 * operand + g
                nc.vector.quantize_mx(
                    out=moving_codes[:, k_pass, :].bitcast(FP8X4),
                    scales=moving_scales[:, k_pass, :],
                    in_=grouped[g][:].rearrange("q b t -> q (b t)"),
                )

        def grouped_tile():
            return grouped_pool.tile([P, HALF, PACK], BF16, name="grouped", tag="grouped", align_bytes=64)

        def regroup_copy(copy, grouped_part, raw_part):
            copy(
                out=grouped_part.rearrange("q (n i) t -> q n t i", i=8),
                in_=raw_part.rearrange("q t (n i) -> q n t i", i=8),
            )

        def regroup(unit, split):
            group, k_pass = units[unit]
            gate, first_tile, tiles = GROUPS[group]
            raw = raw_chunks[(gate * PASSES + k_pass, first_tile // (TILES // 2))]
            first = first_tile * P % HALF
            width = tiles * P
            grouped = grouped_tile()
            if split > 0:
                regroup_copy(nc.vector.tensor_copy, grouped[:, 0:split, :], raw[:, :, first : first + split])
            if split < width:
                regroup_copy(nc.scalar.copy, grouped[:, split:width, :], raw[:, :, first + split : first + width])
            grouped_units[unit] = grouped

        def quantise(unit):
            width = GROUPS[units[unit][0]][2] * P
            codes = codes_pool.tile([P, HALF], U32, name="codes", tag="codes", align_bytes=64)
            scales = codes_pool.tile([P, HALF], U8, name="scales", tag="scales", align_bytes=64)
            nc.vector.quantize_mx(
                out=codes[:, 0:width].bitcast(FP8X4),
                scales=scales[:, 0:width],
                in_=grouped_units[unit][:, 0:width, :].rearrange("q n t -> q (n t)"),
            )
            stationary[units[unit]] = (codes, scales)

        def multiply(group, j, k_pass):
            codes, scales = stationary[(group, k_pass)]
            if k_pass == 0:
                accumulators[(group, j)] = take_bank([P, BATCH], ("sums", group, j))
            columns = slice(j * P, (j + 1) * P)
            nc.tensor.matmul_mx(
                out=accumulators[(group, j)][:],
                lhsT=codes[:, columns].bitcast(FP8X4),
                lhsT_scale=scales[:, columns],
                rhs=moving_codes[:, k_pass, :].bitcast(FP8X4),
                rhs_scale=moving_scales[:, k_pass, :],
                start=(k_pass == 0),
                stop=(k_pass == PASSES - 1),
            )

        ALL = slice(0, BATCH_TILES)

        def activate(group, j, b=ALL):
            gate, first_tile, tiles = GROUPS[group]
            tile_index = first_tile + j
            rows = slice(b.start * P, b.stop * P)
            if gate == GATE_I:
                result = i_gate[:, tile_index, rows]
            else:
                if b.start == 0:
                    gate_tiles[(group, j)] = gate_pool.tile([P, BATCH], F32, name="gate_tile", tag="gate_tile")
                result = gate_tiles[(group, j)][:, rows]
            bias_index = gate * TILES + tile_index
            nc.scalar.activation(
                out=result,
                in_=accumulators[(group, j)][:, rows],
                func=gate_functions[gate],
                bias=bias_columns[:, bias_index : bias_index + 1],
                scale=1.0,
            )
            if b.stop == BATCH_TILES:
                give_back(("sums", group, j))

        def multiply_by_i(group, j):
            g_tile = gate_tiles[(group, j)]
            tile_index = GROUPS[group][1] + j
            nc.vector.tensor_mul(out=g_tile[:], in0=g_tile[:], in1=i_gate[:, tile_index, :])

        def turn(group, j, b=ALL):
            bank = take_bank([P, BATCH_TILES, P], ("turned", group, j))
            for b_tile in range(b.start, b.stop):
                nc.tensor.transpose(
                    out=bank[:, b_tile, :],
                    in_=gate_tiles[(group, j)][:, b_tile * P : (b_tile + 1) * P],
                    identity=identity[:],
                )
            turned_banks[(group, j)] = bank

        def tile_columns(group, j):
            first = (GROUPS[group][1] + j) * P
            return slice(first, first + P)

        def tile_of_pair(pairs, group, j, b=ALL):
            pair, odd = divmod(GROUPS[group][1] + j, 2)
            return pairs[:, pair, b, odd * P : (odd + 1) * P]

        def combine(group, j, b=ALL):
            gate = GROUPS[group][0]
            turned = turned_banks[(group, j)][:, b, :]
            c_part = tile_of_pair(c_new, group, j, b)
            h_part = tile_of_pair(h_new, group, j, b)
            if gate == GATE_F:
                nc.vector.tensor_mul(out=c_part, in0=turned, in1=c_rows[:, b, tile_columns(group, j)])
            if gate == GATE_G:
                nc.vector.tensor_add(out=c_part, in0=turned, in1=c_part)
            if gate == GATE_O:
                nc.vector.tensor_mul(out=h_part, in0=turned, in1=h_part)
            give_back(("turned", group, j))

        def store(group, j, b=ALL):
            gate = GROUPS[group][0]
            pair = (GROUPS[group][1] + j) // 2
            piece = slice(pair * 2 * P, (pair + 1) * 2 * P)
            if gate == GATE_G:
                nc.sync.dma_start(out=c_new_rows[:, b, piece], in_=c_new[:, pair, b, :])
            if gate == GATE_O:
                nc.sync.dma_start(out=h_new_rows[:, b, piece], in_=h_new[:, pair, b, :])

        def tanh_of_c_new(group, j):
            nc.scalar.activation(
                out=tile_of_pair(h_new, group, j), in_=tile_of_pair(c_new, group, j), func=ACT.Tanh
            )

        def sum_biases():
            nc.vector.tensor_add(out=bias_row_sums[:], in0=bias_rows[:, 0, :], in1=bias_rows[:, 1, :])

        def turn_biases():
            bias_bank = take_bank([P, P], "bias")
            nc.tensor.transpose(out=bias_bank[:], in_=bias_row_sums[:], identity=identity[:])
            return bias_bank

        def keep_biases(bias_bank):
            nc.vector.tensor_copy(out=bias_columns[:], in_=bias_bank[:, 0 : GATES * TILES])
            give_back("bias")

        def pipeline_round(r, extra=0):
            if r < len(units):
                group, k_pass = units[r]
                gate, first_tile, tiles = GROUPS[group]
                width = tiles * P
                split = VECTOR_SHARE[group] * width // 512 // 16 * 16
                regroup(r, max(0, min(width, split + extra)))
            for group, j in steps_in.get((r, "combine"), []):
                if COMBINE_FIRST:
                    combine_and_store(group, j)
            if 1 <= r <= len(units):
                quantise(r - 1)
            for group, j in steps_in.get((r, "act"), []):
                activate(group, j)
            for group, j in steps_in.get((r, "times_i"), []):
                multiply_by_i(group, j)
            for group, j in steps_in.get((r, "turn"), []):
                turn(group, j)
            for group, j in steps_in.get((r, "combine"), []):
                if not COMBINE_FIRST:
                    combine_and_store(group, j)
            for group, j in steps_in.get((r, "tanh"), []):
                tanh_of_c_new(group, j)
            for group, j, k_pass in steps_in.get((r, "pass"), []):
                multiply(group, j, k_pass)

        def combine_and_store(group, j):
            combine(group, j)
            if (GROUPS[group][1] + j) % STORE_TILES == STORE_TILES - 1:
                store(group, j)

        def last_tiles():
            group = len(GROUPS) - 1
            tiles = GROUPS[group][2]
            halves = [slice(0, 2), slice(2, 4)]
            for b in halves:
                for j in range(tiles):
                    activate(group, j, b)
            for b in halves:
                for j in range(tiles):
                    turn(group, j, b)
                    combine(group, j, b)
                store(group, tiles - 1, b)

        with tc.manual_schedule():
            make_identity(nc, identity[:])
            nc.vector.memset(table_warmer[:], 0.0)
            nc.scalar.activation(out=table_warmer[:], in_=table_warmer[:], func=ACT.Sigmoid)
            nc.vector.memset(bias_rows[:], 0.0)
            x_rows = raw_pool.tile([P, BATCH_TILES, DIM], BF16, name="raw", tag="raw")
            h_rows = raw_pool.tile([P, BATCH_TILES, DIM], BF16, name="raw", tag="raw")
            load_batch_rows(x_rows, x, 0)
            load_bias(0)
            load_batch_rows(x_rows, x, 2)
            load_bias(1)
            load_chunk(0)
            load_bias(2)
            load_chunk(1)
            load_bias(3)
            nc.sync.dma_start(out=h_rows[:], in_=h.rearrange("(p b) k -> p b k", p=P))
            load_bias(4)
            load_bias(5)
            load_chunk(2)
            load_bias(6)
            load_chunk(3)
            load_bias(7)
            load_chunk(4)
            load_chunk(5)
            x_grouped = [grouped_tile(), grouped_tile()]
            turn_moving(x_rows, x_grouped, 0)
            turn_moving(x_rows, x_grouped, 1)
            quantise_moving(0, x_grouped)
            load_chunk(6)
            pipeline_round(0)
            pipeline_round(1)
            pipeline_round(2, -80)
            h_grouped = [grouped_tile(), grouped_tile()]
            pipeline_round(3)
            turn_moving(h_rows, h_grouped, 0)
            turn_moving(h_rows, h_grouped, 1)
            load_chunk(7)
            load_batch_rows(c_rows, c, 0)
            load_batch_rows(c_rows, c, 2)
            for half in range(2):
                for chunk in range(2 * PASSES, 3 * PASSES):
                    load_half_chunk(chunk, half)
            pipeline_round(4, -80)
            quantise_moving(1, h_grouped)
            for r in range(5, 8):
                pipeline_round(r)
                if r == 5:
                    sum_biases()
                if r == 6:
                    bias_bank = turn_biases()
            keep_biases(bias_bank)
            for chunk in range(3 * PASSES, GATES * PASSES):
                load_chunk(chunk)
            for r in range(8, len(units) + EXTRA_ROUNDS):
                pipeline_round(r)
            last_tiles()
